import numpy as np
import ml_dtypes


def mxq(x, axis, fmt="e4m3"):
    dtype, down = {"e4m3": (ml_dtypes.float8_e4m3fn, 7), "e5m2": (ml_dtypes.float8_e5m2, 14)}[fmt]
    v = np.moveaxis(np.asarray(x, np.float32).astype(ml_dtypes.bfloat16).astype(np.float64), axis, -1)
    blocks = v.reshape(v.shape[:-1] + (-1, 32))
    amax = np.abs(blocks).max(-1, keepdims=True)
    byte = np.maximum(np.where(amax > 0, np.frexp(amax)[1] - 1 + 127, 0) - down, 1)
    scale = np.exp2(byte - 127.0)
    codes = (blocks / scale).astype(np.float32).astype(dtype).astype(np.float64)
    return np.moveaxis((codes * scale).reshape(v.shape), -1, axis)


WIDE = False


def mx_kscale(k):
    if not WIDE:
        return np.ones(k)
    levels = np.array([10, -10, 5, -5, 0])
    if k % 512:
        return np.exp2(np.random.permutation(np.resize(levels, k // 32))).repeat(32)
    a = np.empty((k // 512, 16))
    for p in range(k // 512):
        a[p, :8] = np.random.permutation(np.resize(levels, 8))
        for g in range(8):
            far = levels[np.abs(levels - a[p, g]) >= 10]
            a[p, g + 8] = far[np.random.randint(len(far))]
    return np.exp2(a.ravel()).repeat(32)


BF16 = ml_dtypes.bfloat16


def bf(x):
    return np.asarray(x, np.float32).astype(BF16)


def f64(x):
    return np.asarray(x).astype(np.float64)


E2M1 = np.array([0.0, 0.5, 1.0, 1.5, 2.0, 3.0, 4.0, 6.0, -0.0, -0.5, -1.0, -1.5, -2.0, -3.0, -4.0, -6.0])


def pack_weight(w, fmt):
    k, n = w.shape
    w = f64(bf(w)).reshape(k // 32, 32, n)
    amax = np.abs(w).max(1)
    if fmt == "e4m3":
        byte = np.frexp(amax)[1] - 1 + 127 - 7
    else:
        mant, ex = np.frexp(amax / 6.0)
        byte = np.where(mant > 0.5, ex, ex - 1) + 127
    byte = np.clip(np.where(amax > 0, byte, 1), 1, 254)
    scaled = (w * np.exp2(127.0 - byte)[:, None, :]).reshape(k, n).astype(np.float32)
    by_word = np.ascontiguousarray(scaled.reshape(k // 512, 128, 4, n).transpose(0, 1, 3, 2))
    if fmt == "e4m3":
        words = by_word.astype(ml_dtypes.float8_e4m3fn).view(np.uint8)
    else:
        c = by_word.astype(ml_dtypes.float4_e2m1fn).view(np.uint8) & 0xF
        words = c[..., 0::2] | (c[..., 1::2] << 4)
    return np.ascontiguousarray(words), np.ascontiguousarray(byte.astype(np.uint8).reshape(k // 512, 16, n))


def unpack_weight(words, scales, fmt):
    g, p, n, _ = words.shape
    if fmt == "e4m3":
        vals = np.ascontiguousarray(words).view(ml_dtypes.float8_e4m3fn).astype(np.float64)
    else:
        nib = np.empty((g, p, n, 4), np.uint8)
        nib[..., 0::2] = words & 0xF
        nib[..., 1::2] = words >> 4
        vals = E2M1[nib]
    vals = vals * np.repeat(np.exp2(scales.astype(np.float64) - 127.0), 8, axis=1)[..., None]
    return vals.transpose(0, 1, 3, 2).reshape(g * 512, n)
def pack4(w):
    words, scales = pack_weight(w, "e2m1")
    return words.reshape(words.shape[0], 128, -1), scales


def unpack4(words, scales):
    return unpack_weight(words.reshape(words.shape[0], 128, -1, 2), scales, "e2m1")


N, K, F, H, O, Q, GS, SO = 1024, 8, 1024, 512, 256, 1024, 3, 2


def draw0():
    s, t = mx_kscale(F), mx_kscale(H)
    x = bf(np.random.standard_normal((N, F)) * s)
    contexts = bf(np.random.standard_normal((N, K, F)) * s)
    attn = bf(np.random.random((N, K)))
    Wn_words, Wn_scales = pack4((np.random.standard_normal((H, F)) * 0.5 / np.sqrt(F) / s * t[:, None]).T)
    bn = bf(np.random.standard_normal(H) * 0.1 * t)
    Wc_words, Wc_scales = pack4((np.random.standard_normal((H, F)) * 1.5 / np.sqrt(F) / s * t[:, None]).T)
    bc = bf(np.random.standard_normal(H) * 0.1 * t)
    Wu_words, Wu_scales = pack4((np.random.standard_normal((O, H)) * 1.5 / np.sqrt(H) / t).T)
    bu = bf(np.random.standard_normal(O) * 0.1)
    return {"x": x,
            "contexts": contexts,
            "attn": attn,
            "Wn_words": Wn_words,
            "Wn_scales": Wn_scales,
            "bn": bn,
            "Wc_words": Wc_words,
            "Wc_scales": Wc_scales,
            "bc": bc,
            "Wu_words": Wu_words,
            "Wu_scales": Wu_scales,
            "bu": bu}


def core(x, contexts, attn, Wn_words, Wn_scales, bn, Wc_words, Wc_scales, bc, Wu_words, Wu_scales, bu):
    xt = (mxq(f64(x), 1, "e4m3") @ unpack4(Wn_words, Wn_scales)) + f64(bn)
    ct = (mxq(f64(contexts).reshape(N * K, F), 1, "e4m3") @ unpack4(Wc_words, Wc_scales)).reshape(N, K, H) + f64(bc)
    ca = (ct * f64(attn)[..., None]).mean(axis=1)
    return (mxq(xt + ca, 1, "e4m3") @ unpack4(Wu_words, Wu_scales)) + f64(bu)


def e4m3fn_bytes(y):
    return np.clip(np.asarray(y, np.float64), -448.0, 448.0).astype(np.float32).astype(ml_dtypes.float8_e4m3fn).view(np.uint8)


def e4m3fn_values(b):
    return np.asarray(b, np.uint8).view(ml_dtypes.float8_e4m3fn).astype(np.float64)


def setup_inputs():
    d = draw0()
    x0 = np.asarray(d['contexts']).astype(np.float64)
    s = (np.max(np.abs(x0), axis=(0, 1), keepdims=True) / 448.0).astype(np.float32)
    out = {}
    for k, v in d.items():
        if k == 'contexts':
            out['contexts_bytes'] = e4m3fn_bytes(x0 / s.astype(np.float64))
            out['contexts_scale'] = s
        else:
            out[k] = v
    return out


def reference(x, contexts_bytes, contexts_scale, attn, Wn_words, Wn_scales, bn, Wc_words, Wc_scales, bc, Wu_words, Wu_scales, bu):
    return core(x, e4m3fn_values(contexts_bytes) * contexts_scale.astype(np.float64), attn, Wn_words, Wn_scales, bn, Wc_words, Wc_scales, bc, Wu_words, Wu_scales, bu)

from contextlib import ExitStack

import concourse.mybir as mybir
from concourse.masks import make_identity

F32 = mybir.dt.float32
BF16 = mybir.dt.bfloat16
I32 = mybir.dt.int32
U32 = mybir.dt.uint32
U8 = mybir.dt.uint8
FP8 = mybir.dt.float8_e4m3fn
FP8X4 = mybir.dt.float8_e4m3fn_x4
FP4X4 = mybir.dt.float4_e2m1fn_x4
COPY = mybir.ActivationFunctionType.Copy
ADD = mybir.AluOpType.add
MULT = mybir.AluOpType.mult
AX = mybir.AxisListType.X

NODES, CTX, F, H, O = 1024, 8, 1024, 512, 256
P = 128
LC, ML, CL, GL, HL, QPOS, CAST_FIRST = 3, 2, 1, 1, 6, 1, True
GS = 1
BW, BC, BCT = 5, 4, 3
TILES = NODES // P
FLOPS = 2 * NODES * CTX * F * H + 2 * NODES * F * H + 2 * NODES * H * O


def tile_nodeembeddinglayer_pa_t_w4_kernel(
    tc, x, contexts_bytes, contexts_scale, attn, Wn_words, Wn_scales, bn,
    Wc_words, Wc_scales, bc, Wu_words, Wu_scales, bu, out,
):
    nc = tc.nc
    with ExitStack() as ctx:
        keep = ctx.enter_context(tc.tile_pool(name="keep", bufs=1))
        raw_pool = ctx.enter_context(tc.tile_pool(name="raw", bufs=16))
        work = ctx.enter_context(tc.tile_pool(name="work", bufs=3))
        psum = ctx.enter_context(tc.psum_pool(name="psum", bufs=2))
        ctx.enter_context(tc.manual_schedule())

        csc = keep.tile([P, 2, 1, 2, 2], F32)
        ident = keep.tile([P, P], F32)
        scl = keep.tile([P, 2304], U8, align_bytes=64)
        wc = keep.tile([P, 2, 1024], U8, align_bytes=64)
        wn = keep.tile([P, 2, 1024], U8, align_bytes=64)
        wu = keep.tile([P, 512], U8, align_bytes=64)
        attn_bf = keep.tile([P, TILES, CTX], BF16)
        attn_s = keep.tile([P, TILES, CTX], F32)
        asum = keep.tile([P, TILES], F32)
        bc_b = keep.tile([P, H], BF16)
        bn_b = keep.tile([P, H], BF16)
        bu_b = keep.tile([P, O], BF16)
        bias = keep.tile([P, TILES, H], F32)
        warm = keep.tile([P, 2], F32)

        nc.vector.memset(warm[:], 0.0)
        nc.scalar.activation(out=warm[:, 0:1], in_=warm[:, 1:2], func=COPY)
        nc.vector.memset(scl[:].bitcast(I32), 0)
        make_identity(nc, ident[:])

        raws = {}
        xs = {}

        def load_ctx(i, half, cuts):
            t = raw_pool.tile([P, 4096], U8, name="ctx_raw")
            step = 4096 // cuts
            for q in range(cuts):
                k0 = 4 * half + 4 * q // cuts
                nc.sync.dma_start(
                    out=t[:, step * q : step * (q + 1)],
                    in_=contexts_bytes[P * i : P * (i + 1), k0 : k0 + 4 // cuts, :].rearrange("n k f -> n (k f)"),
                )
            raws[(i, half)] = t

        def load_x(i):
            t = raw_pool.tile([P, 2, F], BF16, name="x_raw", bufs=4)
            nc.sync.dma_start(out=t[:], in_=x[2 * P * i : 2 * P * (i + 1), :].rearrange("(c p) f -> p c f", p=P))
            xs[i] = t

        def load_scales(src, c0, n, groups):
            for q in range(4):
                nc.sync.dma_start(
                    out=scl[32 * q : 32 * q + 4, c0 : c0 + groups * n].rearrange("p (g n) -> p g n", g=groups).bitcast(I32),
                    in_=src[:, 4 * q : 4 * q + 4, :].rearrange("g q n -> q g n").bitcast(I32),
                )

        load_ctx(0, 0, 2)
        nc.sync.dma_start(
            out=csc[:].rearrange("p g o u e -> p (g o) (u e)"),
            in_=contexts_scale.rearrange("a b (g p t) -> p (a b g) t", p=P, t=4),
        )
        nc.sync.dma_start(out=wc[:], in_=Wc_words.rearrange("g p n -> p g n"))
        load_x(0)
        load_scales(Wc_scales, 0, 512, 2)
        load_scales(Wn_scales, 1024, 512, 2)
        load_scales(Wu_scales, 2048, 256, 1)
        load_ctx(0, 1, 1)
        nc.sync.dma_start(out=wn[:], in_=Wn_words.rearrange("g p n -> p g n"))
        nc.sync.dma_start(out=attn_bf[:], in_=attn.rearrange("(i p) k -> p i k", p=P))
        nc.sync.dma_start(out=bc_b[:], in_=bc.partition_broadcast(P))
        nc.sync.dma_start(out=bn_b[:], in_=bn.partition_broadcast(P))
        load_ctx(1, 0, 1)
        load_ctx(1, 1, 1)
        nc.sync.dma_start(out=bu_b[:], in_=bu.partition_broadcast(P))
        nc.sync.dma_start(out=wu[:], in_=Wu_words.rearrange("g p n -> p (g n)"))
        for i in range(2, TILES):
            if i % 2 == 0:
                load_x(i // 2)
            load_ctx(i, 0, 1)
            load_ctx(i, 1, 1)

        chunks = []
        for i in range(TILES):
            if i % 2 == 0 and i > 0:
                chunks.append(("x", i // 2, 0))
            for j in range(4):
                chunks.append(("c", i, j))
                if i == 0 and j == 0:
                    chunks.append(("x", 0, 0))
        n = len(chunks)
        wide, turned, grouped, coded, sums, scaled, xtb, acc, hs = {}, {}, {}, {}, {}, {}, {}, {}, {}
        hturned, hcodes, hsum = {}, {}, {}

        def widen(s):
            kind, i, j = chunks[s]
            if kind == "x":
                wide[s] = xs[i]
                return
            w = work.tile([P, 2, F], BF16, name="wide", bufs=BW)
            src = raws[(i, j // 2)][:, 2048 * (j % 2) : 2048 * (j % 2 + 1)]
            if s == 0:
                nc.scalar.copy(out=w[:, 0, :], in_=src[:, 0:1024].bitcast(FP8))
                nc.vector.tensor_copy(out=w[:, 1, :], in_=src[:, 1024:2048].bitcast(FP8))
            else:
                nc.scalar.copy(out=w[:].rearrange("p c f -> p (c f)"), in_=src.bitcast(FP8))
            wide[s] = w

        def turn(s):
            for g in range(2):
                t = psum.tile([P, 2, 256], F32, name="turned%d" % g, bufs=2)
                for c in range(2):
                    words = wide[s][:, c, :].bitcast(F32)
                    for u in range(2):
                        nc.tensor.transpose(t[:, u, P * c : P * (c + 1)], words[:, 256 * g + u : 256 * (g + 1) : 2], ident[:])
                turned[(s, g)] = t

        def empty(s, g):
            kind = chunks[s][0]
            if g == 0:
                grouped[s] = work.tile([P, 2, 1024], BF16, name="grouped", bufs=3, align_bytes=64)
            dst = grouped[s][:, g, :]
            t = turned[(s, g)][:].rearrange("p u r -> p (u r)")
            if kind == "x":
                nc.scalar.copy(out=dst.bitcast(F32).rearrange("p (r u) -> p r u", u=2), in_=t.rearrange("p (u r) -> p r u", u=2))
            else:
                nc.vector.tensor_tensor(
                    out=dst.rearrange("p (r u e) -> p r u e", u=2, e=2),
                    in0=t.bitcast(BF16).rearrange("p (u r e) -> p r u e", u=2, e=2),
                    in1=csc[:, g].to_broadcast([P, 256, 2, 2]),
                    op=MULT,
                )

        def quant(s):
            codes = work.tile([P, 512], U32, name="codes", bufs=BC, align_bytes=64)
            plane = work.tile([P, 512], U8, name="plane", bufs=BC, align_bytes=64)
            nc.vector.quantize_mx(out=codes[:].bitcast(FP8X4), scales=plane[:], in_=grouped[s][:].rearrange("p g c -> p (g c)"))
            coded[s] = (codes, plane)

        def multiply(s):
            kind = chunks[s][0]
            words, s0 = (wc, 0) if kind == "c" else (wn, 1024)
            codes, plane = coded[s]
            for c in range(2):
                ps = psum.tile([P, H], F32, name="ct", bufs=BCT)
                for g in range(2):
                    cols = slice(256 * g + P * c, 256 * g + P * (c + 1))
                    nc.tensor.matmul_mx(
                        out=ps[:], lhsT=codes[:, cols].bitcast(FP8X4), lhsT_scale=plane[:, cols],
                        rhs=words[:, g, :].bitcast(FP4X4), rhs_scale=scl[:, s0 + 512 * g : s0 + 512 * (g + 1)],
                        start=(g == 0), stop=(g == 1),
                    )
                sums[(s, c)] = ps

        last_chunk = n - 1

        def weigh(s):
            kind, i, j = chunks[s]
            for c in range(2):
                ps = sums[(s, c)]
                if kind == "x":
                    t = work.tile([P, H], F32, name="xtb", bufs=4)
                    nc.vector.tensor_tensor(out=t[:], in0=ps[:], in1=bias[:, 2 * i + c, :], op=ADD)
                    xtb[2 * i + c] = t
                elif s != last_chunk:
                    k = 2 * j + c
                    t = work.tile([P, H], F32, name="scaled", bufs=8)
                    nc.scalar.activation(out=t[:], in_=ps[:], func=COPY, scale=attn_s[:, i, k : k + 1])
                    scaled[(s, c)] = t

        def gather(s):
            kind, i, j = chunks[s]
            if kind == "x":
                return
            if s == last_chunk:
                prev = acc[i]
                for c in range(2):
                    k = 2 * j + c
                    if c == 1:
                        t = work.tile([P, H], BF16, name="h", bufs=2)
                    else:
                        t = work.tile([P, H], F32, name="acc", bufs=3)
                    nc.vector.scalar_tensor_tensor(
                        out=t[:], in0=sums[(s, c)][:], scalar=attn_s[:, i, k : k + 1], in1=prev[:], op0=MULT, op1=ADD)
                    prev = t
                hs[i] = prev
                return
            pair = work.tile([P, H], F32, name="pair", bufs=3)
            for q in range(GS):
                w = slice(H // GS * q, H // GS * (q + 1))
                nc.gpsimd.tensor_tensor(out=pair[:, w], in0=scaled[(s, 0)][:, w], in1=scaled[(s, 1)][:, w], op=ADD)
            if j < 3:
                t = work.tile([P, H], F32, name="acc", bufs=3)
            else:
                t = work.tile([P, H], BF16, name="h", bufs=2)
            prev = xtb[i] if j == 0 else acc[i]
            for q in range(GS):
                w = slice(H // GS * q, H // GS * (q + 1))
                nc.gpsimd.tensor_tensor(out=t[:, w], in0=prev[:, w], in1=pair[:, w], op=ADD)
            acc[i] = t
            if j == 3:
                hs[i] = t

        def h_turn(i):
            t = psum.tile([P, 2, P], F32, name="misc", bufs=1)
            words = hs[i][:].bitcast(F32)
            for u in range(2):
                nc.tensor.transpose(t[:, u, :], words[:, u : 256 : 2], ident[:])
            g = work.tile([P, 512], BF16, name="hgrouped", bufs=2, align_bytes=64)
            nc.scalar.copy(out=g[:].bitcast(F32).rearrange("p (r u) -> p r u", u=2), in_=t[:].rearrange("p u r -> p r u"))
            hturned[i] = g

        def h_quant(i):
            codes = work.tile([P, P], U32, name="hcodes", bufs=2, align_bytes=64)
            plane = work.tile([P, P], U8, name="hplane", bufs=2, align_bytes=64)
            nc.vector.quantize_mx(out=codes[:].bitcast(FP8X4), scales=plane[:], in_=hturned[i][:])
            hcodes[i] = (codes, plane)

        def h_multiply(i):
            codes, plane = hcodes[i]
            ps = psum.tile([P, O], F32, name="misc", bufs=1)
            nc.tensor.matmul_mx(
                out=ps[:], lhsT=codes[:].bitcast(FP8X4), lhsT_scale=plane[:],
                rhs=wu[:].bitcast(FP4X4), rhs_scale=scl[:, 2048:2304], start=True, stop=True)
            hsum[i] = ps

        def h_store(i):
            o = work.tile([P, O], F32, name="o", bufs=2)
            nc.vector.tensor_tensor(out=o[:], in0=hsum[i][:], in1=bu_b[:], op=ADD)
            nc.sync.dma_start(out=out[P * i : P * (i + 1), :], in_=o[:])

        ends = {}
        for s in range(n):
            if chunks[s][0] == "c" and chunks[s][2] == 3:
                ends[s] = chunks[s][1]

        nc.vector.tensor_scalar(out=attn_s[:], in0=attn_bf[:], scalar1=0.125, scalar2=None, op0=MULT)
        for s in range(LC):
            widen(s)
        for i in range(TILES):
            if i == 0:
                nc.vector.tensor_reduce(out=asum[:], in_=attn_s[:], axis=AX, op=ADD)
            nc.gpsimd.tensor_scalar(out=bias[:, i, :], in0=bc_b[:], scalar1=asum[:, i : i + 1], scalar2=0.0, op0=MULT, op1=ADD)
            nc.gpsimd.tensor_tensor(out=bias[:, i, :], in0=bias[:, i, :], in1=bn_b[:], op=ADD)
        turn(0)
        for s in range(n + 12):
            if s + LC < n and CAST_FIRST:
                widen(s + LC)
            if 0 <= s - ML - CL < n and chunks[s - ML - CL][0] == "c":
                weigh(s - ML - CL)
            if s + LC < n and not CAST_FIRST:
                widen(s + LC)
            if s + 1 < n:
                turn(s + 1)
            if s - HL in ends:
                h_turn(ends[s - HL])
            if QPOS == 0 and 0 <= s - 1 < n:
                quant(s - 1)
            if s < n:
                empty(s, 0)
            if QPOS == 1 and 0 <= s - 1 < n:
                quant(s - 1)
            if s < n:
                empty(s, 1)
            if s - HL - 1 in ends:
                h_quant(ends[s - HL - 1])
            if 0 <= s - ML - CL < n and chunks[s - ML - CL][0] == "x":
                weigh(s - ML - CL)
            if s - HL - 2 in ends:
                h_store(ends[s - HL - 2])
            if 0 <= s - ML < n:
                multiply(s - ML)
            if s - HL - 1 in ends:
                h_multiply(ends[s - HL - 1])
            if 0 <= s - ML - CL - GL < n:
                gather(s - ML - CL - GL)
